import numpy as np
import ml_dtypes


def mxq(x, axis, fmt="e4m3"):
    dtype, down = {"e4m3": (ml_dtypes.float8_e4m3fn, 7), "e5m2": (ml_dtypes.float8_e5m2, 14)}[fmt]
    v = np.moveaxis(np.asarray(x, np.float32).astype(ml_dtypes.bfloat16).astype(np.float64), axis, -1)
    blocks = v.reshape(v.shape[:-1] + (-1, 32))
    amax = np.abs(blocks).max(-1, keepdims=True)
    byte = np.maximum(np.where(amax > 0, np.frexp(amax)[1] - 1 + 127, 0) - down, 1)
    scale = np.exp2(byte - 127.0)
    codes = (blocks / scale).astype(np.float32).astype(dtype).astype(np.float64)
    return np.moveaxis((codes * scale).reshape(v.shape), -1, axis)


WIDE = False


def mx_kscale(k):
    if not WIDE:
        return np.ones(k)
    levels = np.array([10, -10, 5, -5, 0])
    if k % 512:
        return np.exp2(np.random.permutation(np.resize(levels, k // 32))).repeat(32)
    a = np.empty((k // 512, 16))
    for p in range(k // 512):
        a[p, :8] = np.random.permutation(np.resize(levels, 8))
        for g in range(8):
            far = levels[np.abs(levels - a[p, g]) >= 10]
            a[p, g + 8] = far[np.random.randint(len(far))]
    return np.exp2(a.ravel()).repeat(32)


BF16 = ml_dtypes.bfloat16


def bf(x):
    return np.asarray(x, np.float32).astype(BF16)


def f64(x):
    return np.asarray(x).astype(np.float64)


N, E, C = 2048, 1024, 512
DENSITY = 0.01
HE_RMS = np.sqrt(np.e / E)


def setup_inputs():
    s, t = mx_kscale(E), mx_kscale(C)
    member = np.random.uniform(size=(N, E)) < DENSITY
    return {"incidence": bf(member * s[None, :]),
            "he": bf(np.random.standard_normal((E, C)) * HE_RMS / s[:, None] * t[None, :]),
            "W2": bf(np.random.standard_normal((C, C)) * 3.0 / np.sqrt(C) / t[:, None]),
            "b2": bf(np.random.standard_normal(C) * 0.2),
            "node_features": bf(np.random.standard_normal((N, C)))}


def reference(incidence, he, W2, b2, node_features):
    prop = mxq(f64(incidence), 1, "e4m3") @ mxq(f64(he), 0, "e4m3")
    return (mxq(prop, 1, "e4m3") @ mxq(f64(W2), 0, "e4m3")) + f64(b2) + f64(node_features)

@@ -1,0 +1,248 @@
+from contextlib import ExitStack
+
+import concourse.mybir as mybir
+from concourse.masks import make_identity
+
+F32 = mybir.dt.float32
+BF16 = mybir.dt.bfloat16
+U32 = mybir.dt.uint32
+U8 = mybir.dt.uint8
+I32 = mybir.dt.int32
+FP8X4 = mybir.dt.float8_e4m3fn_x4
+ADD = mybir.AluOpType.add
+
+P = 128
+N, E, C = 2048, 1024, 512
+NT = N // P
+GT = 2
+NG = NT // GT
+EP = E // 512
+CT = C // P
+
+FLOPS = 2 * N * E * C + 2 * N * C * C
+
+MANUAL = True
+
+
+def tile_heterogeneoustemporalhypergraphnn_pb_kernel(tc, incidence, he, W2, b2, node_features, out):
+    nc = tc.nc
+    with ExitStack() as ctx:
+        if MANUAL:
+            ctx.enter_context(tc.manual_schedule())
+        const = ctx.enter_context(tc.tile_pool(name="const", bufs=1))
+        work = ctx.enter_context(tc.tile_pool(name="work", bufs=3))
+        ps_xt = ctx.enter_context(tc.psum_pool(name="ps_xt", bufs=3))
+        ps_pt = ctx.enter_context(tc.psum_pool(name="ps_pt", bufs=2))
+        ps_po = ctx.enter_context(tc.psum_pool(name="ps_po", bufs=3))
+
+        inc_v = incidence.rearrange("(p r) e -> p r e", r=NT)
+        nf_v = node_features.rearrange("(p r) c -> p r c", r=NT)
+        out_v = out.rearrange("(p r) c -> p r c", r=NT)
+
+        ident = const.tile([P, P], F32)
+        make_identity(nc, ident[:])
+        ones = const.tile([P, P], BF16)
+        nc.vector.memset(ones[:], 1.0)
+        b2pad = const.tile([P, C], BF16)
+        nc.vector.memset(b2pad[:].bitcast(I32), 0)
+
+        he_raw = const.tile([P, EP, 4, C], BF16)
+        he_v = he.rearrange("(g q t) c -> q g t c", g=EP, q=P, t=4)
+
+        def load_he(g):
+            nc.sync.dma_start(out=he_raw[:, g], in_=he_v[:, g])
+
+        inc_raw = []
+        nf_raw = []
+        w2_raw = const.tile([P, CT, C], BF16)
+
+        def load_inc(j):
+            t = const.tile([P, GT, E], BF16, name="inc_raw%d" % j)
+            nc.sync.dma_start(out=t[:], in_=inc_v[:, GT * j : GT * (j + 1), :])
+            inc_raw.append(t)
+
+        def load_nf(k):
+            t = const.tile([P, 4, C], BF16, name="nf_raw%d" % k)
+            nc.sync.dma_start(out=t[:], in_=nf_v[:, 4 * k : 4 * (k + 1), :])
+            nf_raw.append(t)
+
+        load_he(0)
+        load_inc(0)
+        nc.sync.dma_start(out=b2pad[0:1, :], in_=b2.rearrange("(o c) -> o c", o=1))
+        load_he(1)
+        load_nf(0)
+        load_inc(1)
+        nc.sync.dma_start(out=w2_raw[:], in_=W2.rearrange("(p t) n -> p t n", t=CT))
+        load_inc(2)
+        load_inc(3)
+        load_nf(1)
+        load_inc(4)
+        load_inc(5)
+        load_nf(2)
+        load_inc(6)
+        load_inc(7)
+        load_nf(3)
+
+        b2bc = const.tile([P, C], F32)
+
+        def spread_bias():
+            b2ps = ps_po.tile([P, C], F32, tag="po")
+            nc.tensor.matmul(b2ps[:], lhsT=ones[:], rhs=b2pad[:], start=True, stop=True)
+            nc.scalar.copy(out=b2bc[:], in_=b2ps[:])
+
+        he_grp = const.tile([P, EP, C, 4], BF16, align_bytes=64)
+        he_codes = const.tile([P, EP, C], U32, align_bytes=64)
+        he_scales = const.tile([P, EP, C], U8, align_bytes=64)
+        for g in range(EP):
+            nc.vector.tensor_copy(
+                out=he_grp[:, g].rearrange("p (u m) t -> p u m t", u=CT),
+                in_=he_raw[:, g].rearrange("p t (m u) -> p u m t", u=CT),
+            )
+        for g in range(EP):
+            nc.vector.quantize_mx(
+                out=he_codes[:, g].bitcast(FP8X4),
+                scales=he_scales[:, g],
+                in_=he_grp[:, g].rearrange("p c t -> p (c t)"),
+            )
+
+        w2_grp = const.tile([P, C, 4], BF16, align_bytes=64)
+        w2_codes = const.tile([P, C], U32, align_bytes=64)
+        w2_scales = const.tile([P, C], U8, align_bytes=64)
+
+        def regroup_w2():
+            nc.vector.tensor_copy(
+                out=w2_grp[:].rearrange("p (c i) t -> p c t i", i=4),
+                in_=w2_raw[:].rearrange("p t (c i) -> p c t i", i=4),
+            )
+
+        def quantise_w2():
+            nc.vector.quantize_mx(
+                out=w2_codes[:].bitcast(FP8X4),
+                scales=w2_scales[:],
+                in_=w2_grp[:].rearrange("p c t -> p (c t)"),
+            )
+
+        inc_grp = {}
+        inc_codes = {}
+        inc_scales = {}
+        prop_ps = {}
+        prop_grp = {}
+        prop_codes = {}
+        prop_scales = {}
+        out_ps = {}
+        nfb = {}
+
+        def transpose_group(j):
+            grp = work.tile([P, GT, EP, P, 4], BF16, tag="inc_grp", align_bytes=64)
+            inc_grp[j] = grp
+            banks = []
+            for a in range(GT):
+                xt = ps_xt.tile([P, 2 * EP, P], F32, tag="xt")
+                words = inc_raw[j][:, a, :].bitcast(F32)
+                for g in range(EP):
+                    for u in range(2):
+                        nc.tensor.transpose(xt[:, 2 * g + u, :], words[:, 256 * g + u : 256 * (g + 1) : 2], ident[:])
+                banks.append(xt)
+            for a in range(GT):
+                nc.scalar.copy(
+                    out=grp[:, a].bitcast(F32),
+                    in_=banks[a][:].rearrange("p (g u) n -> p g n u", u=2),
+                )
+
+        def quantise_inc(j):
+            codes = work.tile([P, GT, EP, P], U32, tag="inc_codes", align_bytes=64)
+            scales = work.tile([P, GT, EP, P], U8, tag="inc_scales", align_bytes=64)
+            inc_codes[j] = codes
+            inc_scales[j] = scales
+            nc.vector.quantize_mx(
+                out=codes[:].rearrange("p a g n -> p (a g n)").bitcast(FP8X4),
+                scales=scales[:].rearrange("p a g n -> p (a g n)"),
+                in_=inc_grp[j][:].rearrange("p a g n t -> p (a g n t)"),
+            )
+
+        def stage1(j):
+            grp = work.tile([P, GT, P, 4], BF16, tag="prop_grp", align_bytes=64)
+            prop_grp[j] = grp
+            banks = []
+            for a in range(GT):
+                pt = ps_pt.tile([P, CT, P], F32, tag="pt")
+                for t in range(CT):
+                    for g in range(EP):
+                        nc.tensor.matmul_mx(
+                            out=pt[:, t, :],
+                            lhsT=he_codes[:, g, P * t : P * (t + 1)].bitcast(FP8X4),
+                            lhsT_scale=he_scales[:, g, P * t : P * (t + 1)],
+                            rhs=inc_codes[j][:, a, g, :].bitcast(FP8X4),
+                            rhs_scale=inc_scales[j][:, a, g, :],
+                            start=(g == 0),
+                            stop=(g == EP - 1),
+                        )
+                banks.append(pt)
+            for a in range(GT):
+                nc.scalar.copy(out=grp[:, a], in_=banks[a][:].rearrange("p t n -> p n t"))
+
+        def quantise_prop(j):
+            codes = work.tile([P, GT, P], U32, tag="prop_codes", align_bytes=64)
+            scales = work.tile([P, GT, P], U8, tag="prop_scales", align_bytes=64)
+            prop_codes[j] = codes
+            prop_scales[j] = scales
+            nc.vector.quantize_mx(
+                out=codes[:].rearrange("p a n -> p (a n)").bitcast(FP8X4),
+                scales=scales[:].rearrange("p a n -> p (a n)"),
+                in_=prop_grp[j][:].rearrange("p a n t -> p (a n t)"),
+            )
+
+        def stage2(j):
+            banks = []
+            for a in range(GT):
+                po = ps_po.tile([P, C], F32, tag="po")
+                nc.tensor.matmul_mx(
+                    out=po[:],
+                    lhsT=prop_codes[j][:, a, :].bitcast(FP8X4),
+                    lhsT_scale=prop_scales[j][:, a, :],
+                    rhs=w2_codes[:].bitcast(FP8X4),
+                    rhs_scale=w2_scales[:],
+                    start=True,
+                    stop=True,
+                )
+                banks.append(po)
+            out_ps[j] = banks
+
+        def pre_add(j):
+            t = const.tile([P, GT, C], F32, name="nfb%d" % j)
+            nfb[j] = t
+            k, h = divmod(j, 2)
+            for a in range(GT):
+                eng = nc.gpsimd if a == 1 else nc.vector
+                eng.tensor_tensor(out=t[:, a, :], in0=nf_raw[k][:, GT * h + a, :], in1=b2bc[:], op=ADD)
+
+        def finish(j):
+            res = const.tile([P, GT, C], F32, name="res%d" % j)
+            for a in range(GT):
+                nc.vector.tensor_tensor(out=res[:, a, :], in0=out_ps[j][a][:], in1=nfb[j][:, a, :], op=ADD)
+                if j == NG - 1:
+                    nc.sync.dma_start(out=out_v[:, GT * j + a, :], in_=res[:, a, :])
+            if j < NG - 1:
+                nc.sync.dma_start(out=out_v[:, GT * j : GT * (j + 1), :], in_=res[:])
+
+        for j in range(NG + 2):
+            if j < NG:
+                transpose_group(j)
+            if j == 0:
+                spread_bias()
+            if 0 <= j - 1 < NG:
+                stage1(j - 1)
+            if 0 <= j - 2 < NG:
+                stage2(j - 2)
+            if j < NG:
+                quantise_inc(j)
+            if j < NG:
+                pre_add(j)
+            if j == 0:
+                regroup_w2()
+            if j == 1:
+                quantise_w2()
+            if 0 <= j - 1 < NG:
+                quantise_prop(j - 1)
+            if 0 <= j - 2 < NG:
+                finish(j - 2)

@@ -21,16 +21,13 @@ CT = C // P
 
 FLOPS = 2 * N * E * C + 2 * N * C * C
 
-MANUAL = True
-
 
 def tile_heterogeneoustemporalhypergraphnn_pb_kernel(tc, incidence, he, W2, b2, node_features, out):
     nc = tc.nc
     with ExitStack() as ctx:
-        if MANUAL:
-            ctx.enter_context(tc.manual_schedule())
+        ctx.enter_context(tc.manual_schedule())
         const = ctx.enter_context(tc.tile_pool(name="const", bufs=1))
-        work = ctx.enter_context(tc.tile_pool(name="work", bufs=3))
+        work = ctx.enter_context(tc.tile_pool(name="work", bufs=4))
         ps_xt = ctx.enter_context(tc.psum_pool(name="ps_xt", bufs=3))
         ps_pt = ctx.enter_context(tc.psum_pool(name="ps_pt", bufs=2))
         ps_po = ctx.enter_context(tc.psum_pool(name="ps_po", bufs=3))
@@ -48,13 +45,12 @@ def tile_heterogeneoustemporalhypergraphnn_pb_kernel(tc, incidence, he, W2, b2, 
 
         he_raw = const.tile([P, EP, 4, C], BF16)
         he_v = he.rearrange("(g q t) c -> q g t c", g=EP, q=P, t=4)
-
-        def load_he(g):
-            nc.sync.dma_start(out=he_raw[:, g], in_=he_v[:, g])
-
         inc_raw = []
         nf_raw = []
         w2_raw = const.tile([P, CT, C], BF16)
+
+        def load_he(g):
+            nc.sync.dma_start(out=he_raw[:, g], in_=he_v[:, g])
 
         def load_inc(j):
             t = const.tile([P, GT, E], BF16, name="inc_raw%d" % j)
@@ -67,16 +63,16 @@ def tile_heterogeneoustemporalhypergraphnn_pb_kernel(tc, incidence, he, W2, b2, 
             nf_raw.append(t)
 
         load_he(0)
+        load_he(1)
         load_inc(0)
         nc.sync.dma_start(out=b2pad[0:1, :], in_=b2.rearrange("(o c) -> o c", o=1))
-        load_he(1)
-        load_nf(0)
         load_inc(1)
         nc.sync.dma_start(out=w2_raw[:], in_=W2.rearrange("(p t) n -> p t n", t=CT))
         load_inc(2)
         load_inc(3)
-        load_nf(1)
+        load_nf(0)
         load_inc(4)
+        load_nf(1)
         load_inc(5)
         load_nf(2)
         load_inc(6)
@@ -93,12 +89,14 @@ def tile_heterogeneoustemporalhypergraphnn_pb_kernel(tc, incidence, he, W2, b2, 
         he_grp = const.tile([P, EP, C, 4], BF16, align_bytes=64)
         he_codes = const.tile([P, EP, C], U32, align_bytes=64)
         he_scales = const.tile([P, EP, C], U8, align_bytes=64)
-        for g in range(EP):
+
+        def regroup_he(g):
             nc.vector.tensor_copy(
                 out=he_grp[:, g].rearrange("p (u m) t -> p u m t", u=CT),
                 in_=he_raw[:, g].rearrange("p t (m u) -> p u m t", u=CT),
             )
-        for g in range(EP):
+
+        def quantise_he(g):
             nc.vector.quantize_mx(
                 out=he_codes[:, g].bitcast(FP8X4),
                 scales=he_scales[:, g],
@@ -125,28 +123,24 @@ def tile_heterogeneoustemporalhypergraphnn_pb_kernel(tc, incidence, he, W2, b2, 
         inc_grp = {}
         inc_codes = {}
         inc_scales = {}
-        prop_ps = {}
         prop_grp = {}
         prop_codes = {}
         prop_scales = {}
         out_ps = {}
         nfb = {}
 
-        def transpose_group(j):
+        def transpose_pair(j):
             grp = work.tile([P, GT, EP, P, 4], BF16, tag="inc_grp", align_bytes=64)
             inc_grp[j] = grp
-            banks = []
             for a in range(GT):
                 xt = ps_xt.tile([P, 2 * EP, P], F32, tag="xt")
                 words = inc_raw[j][:, a, :].bitcast(F32)
                 for g in range(EP):
                     for u in range(2):
                         nc.tensor.transpose(xt[:, 2 * g + u, :], words[:, 256 * g + u : 256 * (g + 1) : 2], ident[:])
-                banks.append(xt)
-            for a in range(GT):
                 nc.scalar.copy(
                     out=grp[:, a].bitcast(F32),
-                    in_=banks[a][:].rearrange("p (g u) n -> p g n u", u=2),
+                    in_=xt[:].rearrange("p (g u) n -> p g n u", u=2),
                 )
 
         def quantise_inc(j):
@@ -163,7 +157,6 @@ def tile_heterogeneoustemporalhypergraphnn_pb_kernel(tc, incidence, he, W2, b2, 
         def stage1(j):
             grp = work.tile([P, GT, P, 4], BF16, tag="prop_grp", align_bytes=64)
             prop_grp[j] = grp
-            banks = []
             for a in range(GT):
                 pt = ps_pt.tile([P, CT, P], F32, tag="pt")
                 for t in range(CT):
@@ -177,9 +170,7 @@ def tile_heterogeneoustemporalhypergraphnn_pb_kernel(tc, incidence, he, W2, b2, 
                             start=(g == 0),
                             stop=(g == EP - 1),
                         )
-                banks.append(pt)
-            for a in range(GT):
-                nc.scalar.copy(out=grp[:, a], in_=banks[a][:].rearrange("p t n -> p n t"))
+                nc.scalar.copy(out=grp[:, a], in_=pt[:].rearrange("p t n -> p n t"))
 
         def quantise_prop(j):
             codes = work.tile([P, GT, P], U32, tag="prop_codes", align_bytes=64)
@@ -193,7 +184,7 @@ def tile_heterogeneoustemporalhypergraphnn_pb_kernel(tc, incidence, he, W2, b2, 
             )
 
         def stage2(j):
-            banks = []
+            out_ps[j] = []
             for a in range(GT):
                 po = ps_po.tile([P, C], F32, tag="po")
                 nc.tensor.matmul_mx(
@@ -205,44 +196,74 @@ def tile_heterogeneoustemporalhypergraphnn_pb_kernel(tc, incidence, he, W2, b2, 
                     start=True,
                     stop=True,
                 )
-                banks.append(po)
-            out_ps[j] = banks
+                out_ps[j].append(po)
 
-        def pre_add(j):
-            t = const.tile([P, GT, C], F32, name="nfb%d" % j)
-            nfb[j] = t
+        def pre_add(engine, j, a):
+            if j not in nfb:
+                nfb[j] = [const.tile([P, C], F32, name="nfb%d_%d" % (j, k)) for k in range(GT)]
             k, h = divmod(j, 2)
-            for a in range(GT):
-                eng = nc.gpsimd if a == 1 else nc.vector
-                eng.tensor_tensor(out=t[:, a, :], in0=nf_raw[k][:, GT * h + a, :], in1=b2bc[:], op=ADD)
+            engine.tensor_tensor(out=nfb[j][a][:], in0=nf_raw[k][:, GT * h + a, :], in1=b2bc[:], op=ADD)
+
+        def pre_add_beside_finish(j):
+            if j not in nfb:
+                nfb[j] = [const.tile([P, C], F32, name="nfb%d_%d" % (j, k)) for k in range(GT)]
+            nc.vector.memset(nfb[j][1][:, 0:1], 0.0)
+            pre_add(nc.gpsimd, j, 1)
 
         def finish(j):
             res = const.tile([P, GT, C], F32, name="res%d" % j)
             for a in range(GT):
-                nc.vector.tensor_tensor(out=res[:, a, :], in0=out_ps[j][a][:], in1=nfb[j][:, a, :], op=ADD)
+                nc.vector.tensor_tensor(out=res[:, a, :], in0=out_ps[j][a][:], in1=nfb[j][a][:], op=ADD)
                 if j == NG - 1:
                     nc.sync.dma_start(out=out_v[:, GT * j + a, :], in_=res[:, a, :])
             if j < NG - 1:
                 nc.sync.dma_start(out=out_v[:, GT * j : GT * (j + 1), :], in_=res[:])
 
-        for j in range(NG + 2):
-            if j < NG:
-                transpose_group(j)
-            if j == 0:
+        def real(j):
+            return 0 <= j < NG
+
+        for a in range(0, NG + 4, 2):
+            b = a + 1
+            if real(a - 3):
+                pre_add_beside_finish(a - 3)
+            if real(a - 4):
+                finish(a - 4)
+            if real(a):
+                transpose_pair(a)
+            if a == 0:
+                regroup_he(0)
+                regroup_he(1)
+                quantise_he(0)
+                quantise_he(1)
+                quantise_inc(0)
                 spread_bias()
-            if 0 <= j - 1 < NG:
-                stage1(j - 1)
-            if 0 <= j - 2 < NG:
-                stage2(j - 2)
-            if j < NG:
-                quantise_inc(j)
-            if j < NG:
-                pre_add(j)
-            if j == 0:
+            if real(b):
+                transpose_pair(b)
+            if real(a - 2):
+                quantise_prop(a - 2)
+            if real(a) and a > 0:
+                quantise_inc(a)
+            if real(a - 1):
+                pre_add(nc.vector, a - 1, 0)
+            if a == 0:
                 regroup_w2()
-            if j == 1:
+            if real(a - 1):
+                stage1(a - 1)
+            if real(a - 3):
+                stage2(a - 3)
+            if real(b):
+                quantise_inc(b)
+            if a == 0:
                 quantise_w2()
-            if 0 <= j - 1 < NG:
-                quantise_prop(j - 1)
-            if 0 <= j - 2 < NG:
-                finish(j - 2)
+            if real(a):
+                pre_add(nc.vector, a, 0)
+            if real(a - 1):
+                quantise_prop(a - 1)
+            if real(a - 2):
+                pre_add_beside_finish(a - 2)
+            if real(a - 3):
+                finish(a - 3)
+            if real(a):
+                stage1(a)
+            if real(a - 2):
+                stage2(a - 2)

@@ -38,6 +38,8 @@ def tile_heterogeneoustemporalhypergraphnn_pb_kernel(tc, incidence, he, W2, b2, 
 
         ident = const.tile([P, P], F32)
         make_identity(nc, ident[:])
+        ident16 = const.tile([P, P], BF16)
+        make_identity(nc, ident16[:])
         ones = const.tile([P, P], BF16)
         nc.vector.memset(ones[:], 1.0)
         b2pad = const.tile([P, C], BF16)
@@ -62,17 +64,17 @@ def tile_heterogeneoustemporalhypergraphnn_pb_kernel(tc, incidence, he, W2, b2, 
             nc.sync.dma_start(out=t[:], in_=nf_v[:, 4 * k : 4 * (k + 1), :])
             nf_raw.append(t)
 
+        load_inc(0)
         load_he(0)
         load_he(1)
-        load_inc(0)
         nc.sync.dma_start(out=b2pad[0:1, :], in_=b2.rearrange("(o c) -> o c", o=1))
         load_inc(1)
         nc.sync.dma_start(out=w2_raw[:], in_=W2.rearrange("(p t) n -> p t n", t=CT))
         load_inc(2)
-        load_inc(3)
         load_nf(0)
-        load_inc(4)
+        load_inc(3)
         load_nf(1)
+        load_inc(4)
         load_inc(5)
         load_nf(2)
         load_inc(6)
@@ -91,10 +93,11 @@ def tile_heterogeneoustemporalhypergraphnn_pb_kernel(tc, incidence, he, W2, b2, 
         he_scales = const.tile([P, EP, C], U8, align_bytes=64)
 
         def regroup_he(g):
-            nc.vector.tensor_copy(
-                out=he_grp[:, g].rearrange("p (u m) t -> p u m t", u=CT),
-                in_=he_raw[:, g].rearrange("p t (m u) -> p u m t", u=CT),
-            )
+            for copy, cols in ((nc.vector.tensor_copy, slice(0, 80)), (nc.scalar.copy, slice(80, P))):
+                copy(
+                    out=he_grp[:, g].rearrange("p (u m) t -> p u m t", u=CT)[:, :, cols, :],
+                    in_=he_raw[:, g].rearrange("p t (m u) -> p u m t", u=CT)[:, :, cols, :],
+                )
 
         def quantise_he(g):
             nc.vector.quantize_mx(
@@ -198,72 +201,55 @@ def tile_heterogeneoustemporalhypergraphnn_pb_kernel(tc, incidence, he, W2, b2, 
                 )
                 out_ps[j].append(po)
 
-        def pre_add(engine, j, a):
-            if j not in nfb:
-                nfb[j] = [const.tile([P, C], F32, name="nfb%d_%d" % (j, k)) for k in range(GT)]
+        def pre_add_on_tensor(j, a):
             k, h = divmod(j, 2)
-            engine.tensor_tensor(out=nfb[j][a][:], in0=nf_raw[k][:, GT * h + a, :], in1=b2bc[:], op=ADD)
+            ps = ps_xt.tile([P, C], F32, tag="xt")
+            nc.tensor.matmul(ps[:], lhsT=ident16[:], rhs=nf_raw[k][:, GT * h + a, :], start=True, stop=False)
+            nc.tensor.matmul(ps[:], lhsT=ones[:], rhs=b2pad[:], start=False, stop=True)
+            nc.scalar.copy(out=nfb[j][:, a, :], in_=ps[:])
 
-        def pre_add_beside_finish(j):
-            if j not in nfb:
-                nfb[j] = [const.tile([P, C], F32, name="nfb%d_%d" % (j, k)) for k in range(GT)]
-            nc.vector.memset(nfb[j][1][:, 0:1], 0.0)
-            pre_add(nc.gpsimd, j, 1)
+        def pre_add(j, a0, a1):
+            k, h = divmod(j, 2)
+            nc.vector.tensor_tensor(
+                out=nfb[j][:, a0:a1, :],
+                in0=nf_raw[k][:, GT * h + a0 : GT * h + a1, :],
+                in1=b2bc[:].unsqueeze(1).to_broadcast([P, a1 - a0, C]),
+                op=ADD,
+            )
 
         def finish(j):
             res = const.tile([P, GT, C], F32, name="res%d" % j)
             for a in range(GT):
-                nc.vector.tensor_tensor(out=res[:, a, :], in0=out_ps[j][a][:], in1=nfb[j][a][:], op=ADD)
+                nc.vector.tensor_tensor(out=res[:, a, :], in0=out_ps[j][a][:], in1=nfb[j][:, a, :], op=ADD)
                 if j == NG - 1:
                     nc.sync.dma_start(out=out_v[:, GT * j + a, :], in_=res[:, a, :])
             if j < NG - 1:
                 nc.sync.dma_start(out=out_v[:, GT * j : GT * (j + 1), :], in_=res[:])
 
-        def real(j):
-            return 0 <= j < NG
-
-        for a in range(0, NG + 4, 2):
-            b = a + 1
-            if real(a - 3):
-                pre_add_beside_finish(a - 3)
-            if real(a - 4):
-                finish(a - 4)
-            if real(a):
-                transpose_pair(a)
-            if a == 0:
-                regroup_he(0)
-                regroup_he(1)
-                quantise_he(0)
-                quantise_he(1)
-                quantise_inc(0)
-                spread_bias()
-            if real(b):
-                transpose_pair(b)
-            if real(a - 2):
-                quantise_prop(a - 2)
-            if real(a) and a > 0:
-                quantise_inc(a)
-            if real(a - 1):
-                pre_add(nc.vector, a - 1, 0)
-            if a == 0:
+        transpose_pair(0)
+        regroup_he(0)
+        regroup_he(1)
+        quantise_he(0)
+        quantise_inc(0)
+        quantise_he(1)
+        spread_bias()
+        for j in range(NG + 1):
+            if j < NG:
+                nfb[j] = const.tile([P, GT, C], F32, name="nfb%d" % j)
+                if j % 2:
+                    pre_add_on_tensor(j, 0)
+            if j + 1 < NG:
+                transpose_pair(j + 1)
+            if j < NG:
+                stage1(j)
+            if j + 1 < NG:
+                quantise_inc(j + 1)
+            if j == 0:
                 regroup_w2()
-            if real(a - 1):
-                stage1(a - 1)
-            if real(a - 3):
-                stage2(a - 3)
-            if real(b):
-                quantise_inc(b)
-            if a == 0:
                 quantise_w2()
-            if real(a):
-                pre_add(nc.vector, a, 0)
-            if real(a - 1):
-                quantise_prop(a - 1)
-            if real(a - 2):
-                pre_add_beside_finish(a - 2)
-            if real(a - 3):
-                finish(a - 3)
-            if real(a):
-                stage1(a)
-            if real(a - 2):
-                stage2(a - 2)
+            if j > 0:
+                stage2(j - 1)
+                finish(j - 1)
+            if j < NG:
+                quantise_prop(j)
+                pre_add(j, j % 2, GT)

@@ -69,8 +69,8 @@ def tile_heterogeneoustemporalhypergraphnn_pb_kernel(tc, incidence, he, W2, b2, 
         load_he(1)
         nc.sync.dma_start(out=b2pad[0:1, :], in_=b2.rearrange("(o c) -> o c", o=1))
         load_inc(1)
-        nc.sync.dma_start(out=w2_raw[:], in_=W2.rearrange("(p t) n -> p t n", t=CT))
         load_inc(2)
+        nc.sync.dma_start(out=w2_raw[:], in_=W2.rearrange("(p t) n -> p t n", t=CT))
         load_nf(0)
         load_inc(3)
         load_nf(1)
@@ -93,11 +93,10 @@ def tile_heterogeneoustemporalhypergraphnn_pb_kernel(tc, incidence, he, W2, b2, 
         he_scales = const.tile([P, EP, C], U8, align_bytes=64)
 
         def regroup_he(g):
-            for copy, cols in ((nc.vector.tensor_copy, slice(0, 80)), (nc.scalar.copy, slice(80, P))):
-                copy(
-                    out=he_grp[:, g].rearrange("p (u m) t -> p u m t", u=CT)[:, :, cols, :],
-                    in_=he_raw[:, g].rearrange("p t (m u) -> p u m t", u=CT)[:, :, cols, :],
-                )
+            nc.vector.tensor_copy(
+                out=he_grp[:, g].rearrange("p (u m) t -> p m t u", u=CT),
+                in_=he_raw[:, g].rearrange("p t (m u) -> p m t u", u=CT),
+            )
 
         def quantise_he(g):
             nc.vector.quantize_mx(
@@ -228,28 +227,31 @@ def tile_heterogeneoustemporalhypergraphnn_pb_kernel(tc, incidence, he, W2, b2, 
 
         transpose_pair(0)
         regroup_he(0)
-        regroup_he(1)
         quantise_he(0)
+        regroup_he(1)
         quantise_inc(0)
         quantise_he(1)
         spread_bias()
-        for j in range(NG + 1):
-            if j < NG:
-                nfb[j] = const.tile([P, GT, C], F32, name="nfb%d" % j)
-                if j % 2:
-                    pre_add_on_tensor(j, 0)
-            if j + 1 < NG:
-                transpose_pair(j + 1)
+        transpose_pair(1)
+        for j in range(NG + 2):
+            if j + 2 < NG:
+                transpose_pair(j + 2)
             if j < NG:
                 stage1(j)
+            if j >= 2:
+                stage2(j - 2)
             if j + 1 < NG:
                 quantise_inc(j + 1)
             if j == 0:
                 regroup_w2()
+            if j == 1:
                 quantise_w2()
-            if j > 0:
-                stage2(j - 1)
-                finish(j - 1)
+            if j < NG:
+                nfb[j] = const.tile([P, GT, C], F32, name="nfb%d" % j)
+                pre_add(j, 0, GT if j < NG // 2 else 1)
+            if j >= 2:
+                finish(j - 2)
             if j < NG:
                 quantise_prop(j)
-                pre_add(j, j % 2, GT)
+            if NG // 2 <= j < NG:
+                pre_add_on_tensor(j, 1)

@@ -44,6 +44,8 @@ def tile_heterogeneoustemporalhypergraphnn_pb_kernel(tc, incidence, he, W2, b2, 
         nc.vector.memset(ones[:], 1.0)
         b2pad = const.tile([P, C], BF16)
         nc.vector.memset(b2pad[:].bitcast(I32), 0)
+        zeros = const.tile([P, C], BF16)
+        nc.vector.memset(zeros[:].bitcast(I32), 0)
 
         he_raw = const.tile([P, EP, 4, C], BF16)
         he_v = he.rearrange("(g q t) c -> q g t c", g=EP, q=P, t=4)
@@ -59,18 +61,23 @@ def tile_heterogeneoustemporalhypergraphnn_pb_kernel(tc, incidence, he, W2, b2, 
             nc.sync.dma_start(out=t[:], in_=inc_v[:, GT * j : GT * (j + 1), :])
             inc_raw.append(t)
 
+        def load_first(a):
+            nc.sync.dma_start(out=inc_raw[0][:, a, :], in_=inc_v[:, a, :])
+
         def load_nf(k):
             t = const.tile([P, 4, C], BF16, name="nf_raw%d" % k)
             nc.sync.dma_start(out=t[:], in_=nf_v[:, 4 * k : 4 * (k + 1), :])
             nf_raw.append(t)
 
-        load_inc(0)
+        inc_raw.append(const.tile([P, GT, E], BF16, name="inc_raw0"))
+        load_first(0)
         load_he(0)
         load_he(1)
         nc.sync.dma_start(out=b2pad[0:1, :], in_=b2.rearrange("(o c) -> o c", o=1))
+        load_first(1)
         load_inc(1)
-        load_inc(2)
         nc.sync.dma_start(out=w2_raw[:], in_=W2.rearrange("(p t) n -> p t n", t=CT))
+        load_inc(2)
         load_nf(0)
         load_inc(3)
         load_nf(1)
@@ -82,6 +89,11 @@ def tile_heterogeneoustemporalhypergraphnn_pb_kernel(tc, incidence, he, W2, b2, 
         load_nf(3)
 
         b2bc = const.tile([P, C], F32)
+
+        def warm_up(count):
+            for k in range(count):
+                idle = ps_po.tile([P, C], F32, tag="po")
+                nc.tensor.matmul(idle[:], lhsT=ones[:], rhs=zeros[:], start=True, stop=True)
 
         def spread_bias():
             b2ps = ps_po.tile([P, C], F32, tag="po")
@@ -131,19 +143,22 @@ def tile_heterogeneoustemporalhypergraphnn_pb_kernel(tc, incidence, he, W2, b2, 
         out_ps = {}
         nfb = {}
 
+        def transpose_tile(j, a):
+            if a == 0:
+                inc_grp[j] = work.tile([P, GT, EP, P, 4], BF16, tag="inc_grp", align_bytes=64, name="inc_grp")
+            xt = ps_xt.tile([P, 2 * EP, P], F32, tag="xt")
+            words = inc_raw[j][:, a, :].bitcast(F32)
+            for g in range(EP):
+                for u in range(2):
+                    nc.tensor.transpose(xt[:, 2 * g + u, :], words[:, 256 * g + u : 256 * (g + 1) : 2], ident[:])
+            nc.scalar.copy(
+                out=inc_grp[j][:, a].bitcast(F32),
+                in_=xt[:].rearrange("p (g u) n -> p g n u", u=2),
+            )
+
         def transpose_pair(j):
-            grp = work.tile([P, GT, EP, P, 4], BF16, tag="inc_grp", align_bytes=64)
-            inc_grp[j] = grp
             for a in range(GT):
-                xt = ps_xt.tile([P, 2 * EP, P], F32, tag="xt")
-                words = inc_raw[j][:, a, :].bitcast(F32)
-                for g in range(EP):
-                    for u in range(2):
-                        nc.tensor.transpose(xt[:, 2 * g + u, :], words[:, 256 * g + u : 256 * (g + 1) : 2], ident[:])
-                nc.scalar.copy(
-                    out=grp[:, a].bitcast(F32),
-                    in_=xt[:].rearrange("p (g u) n -> p g n u", u=2),
-                )
+                transpose_tile(j, a)
 
         def quantise_inc(j):
             codes = work.tile([P, GT, EP, P], U32, tag="inc_codes", align_bytes=64)
@@ -220,38 +235,42 @@ def tile_heterogeneoustemporalhypergraphnn_pb_kernel(tc, incidence, he, W2, b2, 
             res = const.tile([P, GT, C], F32, name="res%d" % j)
             for a in range(GT):
                 nc.vector.tensor_tensor(out=res[:, a, :], in0=out_ps[j][a][:], in1=nfb[j][:, a, :], op=ADD)
-                if j == NG - 1:
+                if j >= NG - 2:
                     nc.sync.dma_start(out=out_v[:, GT * j + a, :], in_=res[:, a, :])
-            if j < NG - 1:
+            if j < NG - 2:
                 nc.sync.dma_start(out=out_v[:, GT * j : GT * (j + 1), :], in_=res[:])
 
-        transpose_pair(0)
-        regroup_he(0)
-        quantise_he(0)
-        regroup_he(1)
-        quantise_inc(0)
-        quantise_he(1)
+        warm_up(4)
+        transpose_tile(0, 0)
+        warm_up(2)
         spread_bias()
+        transpose_tile(0, 1)
+        regroup_he(0)
+        regroup_he(1)
+        quantise_he(0)
+        quantise_he(1)
+        quantise_inc(0)
         transpose_pair(1)
+        stage1(0)
+        regroup_w2()
+        quantise_inc(1)
+        quantise_w2()
+        quantise_prop(0)
         for j in range(NG + 2):
             if j + 2 < NG:
                 transpose_pair(j + 2)
-            if j < NG:
+            if 0 < j < NG:
                 stage1(j)
             if j >= 2:
                 stage2(j - 2)
-            if j + 1 < NG:
+            if 0 < j and j + 1 < NG:
                 quantise_inc(j + 1)
-            if j == 0:
-                regroup_w2()
-            if j == 1:
-                quantise_w2()
             if j < NG:
                 nfb[j] = const.tile([P, GT, C], F32, name="nfb%d" % j)
                 pre_add(j, 0, GT if j < NG // 2 else 1)
             if j >= 2:
                 finish(j - 2)
-            if j < NG:
+            if 0 < j < NG:
                 quantise_prop(j)
             if NG // 2 <= j < NG:
                 pre_add_on_tensor(j, 1)

@@ -257,11 +257,15 @@ def tile_heterogeneoustemporalhypergraphnn_pb_kernel(tc, incidence, he, W2, b2, 
         quantise_w2()
         quantise_prop(0)
         for j in range(NG + 2):
+            if j == 1:
+                stage1(1)
             if j + 2 < NG:
                 transpose_pair(j + 2)
-            if 0 < j < NG:
+            if j == 1:
+                stage2(0)
+            if 1 < j < NG:
                 stage1(j)
-            if j >= 2:
+            if j > 2:
                 stage2(j - 2)
             if 0 < j and j + 1 < NG:
                 quantise_inc(j + 1)

@@ -18,6 +18,7 @@ GT = 2
 NG = NT // GT
 EP = E // 512
 CT = C // P
+ON_TENSOR = {5: 1, 6: 1, 7: 2}
 
 FLOPS = 2 * N * E * C + 2 * N * C * C
 
@@ -28,9 +29,9 @@ def tile_heterogeneoustemporalhypergraphnn_pb_kernel(tc, incidence, he, W2, b2, 
         ctx.enter_context(tc.manual_schedule())
         const = ctx.enter_context(tc.tile_pool(name="const", bufs=1))
         work = ctx.enter_context(tc.tile_pool(name="work", bufs=4))
-        ps_xt = ctx.enter_context(tc.psum_pool(name="ps_xt", bufs=3))
+        ps_xt = ctx.enter_context(tc.psum_pool(name="ps_xt", bufs=2))
         ps_pt = ctx.enter_context(tc.psum_pool(name="ps_pt", bufs=2))
-        ps_po = ctx.enter_context(tc.psum_pool(name="ps_po", bufs=3))
+        ps_po = ctx.enter_context(tc.psum_pool(name="ps_po", bufs=4))
 
         inc_v = incidence.rearrange("(p r) e -> p r e", r=NT)
         nf_v = node_features.rearrange("(p r) c -> p r c", r=NT)
@@ -104,10 +105,10 @@ def tile_heterogeneoustemporalhypergraphnn_pb_kernel(tc, incidence, he, W2, b2, 
         he_codes = const.tile([P, EP, C], U32, align_bytes=64)
         he_scales = const.tile([P, EP, C], U8, align_bytes=64)
 
-        def regroup_he(g):
-            nc.vector.tensor_copy(
-                out=he_grp[:, g].rearrange("p (u m) t -> p m t u", u=CT),
-                in_=he_raw[:, g].rearrange("p t (m u) -> p m t u", u=CT),
+        def regroup_he(copy, g, m0, m1):
+            copy(
+                out=he_grp[:, g].rearrange("p (u m) t -> p m t u", u=CT)[:, m0:m1],
+                in_=he_raw[:, g].rearrange("p t (m u) -> p m t u", u=CT)[:, m0:m1],
             )
 
         def quantise_he(g):
@@ -231,22 +232,25 @@ def tile_heterogeneoustemporalhypergraphnn_pb_kernel(tc, incidence, he, W2, b2, 
                 op=ADD,
             )
 
-        def finish(j):
-            res = const.tile([P, GT, C], F32, name="res%d" % j)
-            for a in range(GT):
-                nc.vector.tensor_tensor(out=res[:, a, :], in0=out_ps[j][a][:], in1=nfb[j][:, a, :], op=ADD)
-                if j >= NG - 2:
-                    nc.sync.dma_start(out=out_v[:, GT * j + a, :], in_=res[:, a, :])
-            if j < NG - 2:
-                nc.sync.dma_start(out=out_v[:, GT * j : GT * (j + 1), :], in_=res[:])
+        res = {}
+
+        def finish_tile(j, a):
+            if a == 0:
+                res[j] = const.tile([P, GT, C], F32, name="res%d" % j)
+            nc.vector.tensor_tensor(out=res[j][:, a, :], in0=out_ps[j][a][:], in1=nfb[j][:, a, :], op=ADD)
+            if j >= NG - 2:
+                nc.sync.dma_start(out=out_v[:, GT * j + a, :], in_=res[j][:, a, :])
+            elif a == GT - 1:
+                nc.sync.dma_start(out=out_v[:, GT * j : GT * (j + 1), :], in_=res[j][:])
 
         warm_up(4)
         transpose_tile(0, 0)
         warm_up(2)
+        regroup_he(nc.scalar.copy, 1, 80, P)
         spread_bias()
         transpose_tile(0, 1)
-        regroup_he(0)
-        regroup_he(1)
+        regroup_he(nc.vector.tensor_copy, 0, 0, P)
+        regroup_he(nc.vector.tensor_copy, 1, 0, 80)
         quantise_he(0)
         quantise_he(1)
         quantise_inc(0)
@@ -257,24 +261,25 @@ def tile_heterogeneoustemporalhypergraphnn_pb_kernel(tc, incidence, he, W2, b2, 
         quantise_w2()
         quantise_prop(0)
         for j in range(NG + 2):
-            if j == 1:
-                stage1(1)
+            if 0 < j < NG:
+                stage1(j)
             if j + 2 < NG:
                 transpose_pair(j + 2)
-            if j == 1:
-                stage2(0)
-            if 1 < j < NG:
-                stage1(j)
-            if j > 2:
-                stage2(j - 2)
-            if 0 < j and j + 1 < NG:
-                quantise_inc(j + 1)
+            if 0 < j <= NG:
+                stage2(j - 1)
             if j < NG:
                 nfb[j] = const.tile([P, GT, C], F32, name="nfb%d" % j)
-                pre_add(j, 0, GT if j < NG // 2 else 1)
+                on_vector = GT - ON_TENSOR.get(j, 0)
+                for a in range(on_vector, GT):
+                    pre_add_on_tensor(j, a)
+            if 0 < j and j + 1 < NG:
+                quantise_inc(j + 1)
             if j >= 2:
-                finish(j - 2)
+                for a in range(1 if j == NG else 0, GT):
+                    finish_tile(j - 2, a)
+            if j < NG and on_vector:
+                pre_add(j, 0, on_vector)
+            if j == NG - 1:
+                finish_tile(j - 1, 0)
             if 0 < j < NG:
                 quantise_prop(j)
-            if NG // 2 <= j < NG:
-                pre_add_on_tensor(j, 1)

from contextlib import ExitStack

import concourse.mybir as mybir
from concourse.masks import make_identity

F32 = mybir.dt.float32
BF16 = mybir.dt.bfloat16
U32 = mybir.dt.uint32
U8 = mybir.dt.uint8
I32 = mybir.dt.int32
FP8X4 = mybir.dt.float8_e4m3fn_x4
ADD = mybir.AluOpType.add

P = 128
N, E, C = 2048, 1024, 512
NT = N // P
GT = 2
NG = NT // GT
EP = E // 512
CT = C // P
ON_TENSOR = {5: 1, 6: 1, 7: 2}

FLOPS = 2 * N * E * C + 2 * N * C * C


def tile_heterogeneoustemporalhypergraphnn_pb_kernel(tc, incidence, he, W2, b2, node_features, out):
    nc = tc.nc
    with ExitStack() as ctx:
        ctx.enter_context(tc.manual_schedule())
        const = ctx.enter_context(tc.tile_pool(name="const", bufs=1))
        work = ctx.enter_context(tc.tile_pool(name="work", bufs=4))
        ps_xt = ctx.enter_context(tc.psum_pool(name="ps_xt", bufs=2))
        ps_pt = ctx.enter_context(tc.psum_pool(name="ps_pt", bufs=2))
        ps_po = ctx.enter_context(tc.psum_pool(name="ps_po", bufs=4))

        inc_v = incidence.rearrange("(p r) e -> p r e", r=NT)
        nf_v = node_features.rearrange("(p r) c -> p r c", r=NT)
        out_v = out.rearrange("(p r) c -> p r c", r=NT)

        ident = const.tile([P, P], F32)
        make_identity(nc, ident[:])
        ident16 = const.tile([P, P], BF16)
        make_identity(nc, ident16[:])
        ones = const.tile([P, P], BF16)
        nc.vector.memset(ones[:], 1.0)
        b2pad = const.tile([P, C], BF16)
        nc.vector.memset(b2pad[:].bitcast(I32), 0)
        zeros = const.tile([P, C], BF16)
        nc.vector.memset(zeros[:].bitcast(I32), 0)

        he_raw = const.tile([P, EP, 4, C], BF16)
        he_v = he.rearrange("(g q t) c -> q g t c", g=EP, q=P, t=4)
        inc_raw = []
        nf_raw = []
        w2_raw = const.tile([P, CT, C], BF16)

        def load_he(g):
            nc.sync.dma_start(out=he_raw[:, g], in_=he_v[:, g])

        def load_inc(j):
            t = const.tile([P, GT, E], BF16, name="inc_raw%d" % j)
            nc.sync.dma_start(out=t[:], in_=inc_v[:, GT * j : GT * (j + 1), :])
            inc_raw.append(t)

        def load_first(a):
            nc.sync.dma_start(out=inc_raw[0][:, a, :], in_=inc_v[:, a, :])

        def load_nf(k):
            t = const.tile([P, 4, C], BF16, name="nf_raw%d" % k)
            nc.sync.dma_start(out=t[:], in_=nf_v[:, 4 * k : 4 * (k + 1), :])
            nf_raw.append(t)

        inc_raw.append(const.tile([P, GT, E], BF16, name="inc_raw0"))
        load_first(0)
        load_he(0)
        load_he(1)
        nc.sync.dma_start(out=b2pad[0:1, :], in_=b2.rearrange("(o c) -> o c", o=1))
        load_first(1)
        load_inc(1)
        nc.sync.dma_start(out=w2_raw[:], in_=W2.rearrange("(p t) n -> p t n", t=CT))
        load_inc(2)
        load_nf(0)
        load_inc(3)
        load_nf(1)
        load_inc(4)
        load_inc(5)
        load_nf(2)
        load_inc(6)
        load_inc(7)
        load_nf(3)

        b2bc = const.tile([P, C], F32)

        def warm_up(count):
            for k in range(count):
                idle = ps_po.tile([P, C], F32, tag="po")
                nc.tensor.matmul(idle[:], lhsT=ones[:], rhs=zeros[:], start=True, stop=True)

        def spread_bias():
            b2ps = ps_po.tile([P, C], F32, tag="po")
            nc.tensor.matmul(b2ps[:], lhsT=ones[:], rhs=b2pad[:], start=True, stop=True)
            nc.scalar.copy(out=b2bc[:], in_=b2ps[:])

        he_grp = const.tile([P, EP, C, 4], BF16, align_bytes=64)
        he_codes = const.tile([P, EP, C], U32, align_bytes=64)
        he_scales = const.tile([P, EP, C], U8, align_bytes=64)

        def regroup_he(copy, g, m0, m1):
            copy(
                out=he_grp[:, g].rearrange("p (u m) t -> p m t u", u=CT)[:, m0:m1],
                in_=he_raw[:, g].rearrange("p t (m u) -> p m t u", u=CT)[:, m0:m1],
            )

        def quantise_he(g):
            nc.vector.quantize_mx(
                out=he_codes[:, g].bitcast(FP8X4),
                scales=he_scales[:, g],
                in_=he_grp[:, g].rearrange("p c t -> p (c t)"),
            )

        w2_grp = const.tile([P, C, 4], BF16, align_bytes=64)
        w2_codes = const.tile([P, C], U32, align_bytes=64)
        w2_scales = const.tile([P, C], U8, align_bytes=64)

        def regroup_w2():
            nc.vector.tensor_copy(
                out=w2_grp[:].rearrange("p (c i) t -> p c t i", i=4),
                in_=w2_raw[:].rearrange("p t (c i) -> p c t i", i=4),
            )

        def quantise_w2():
            nc.vector.quantize_mx(
                out=w2_codes[:].bitcast(FP8X4),
                scales=w2_scales[:],
                in_=w2_grp[:].rearrange("p c t -> p (c t)"),
            )

        inc_grp = {}
        inc_codes = {}
        inc_scales = {}
        prop_grp = {}
        prop_codes = {}
        prop_scales = {}
        out_ps = {}
        nfb = {}

        def transpose_tile(j, a):
            if a == 0:
                inc_grp[j] = work.tile([P, GT, EP, P, 4], BF16, tag="inc_grp", align_bytes=64, name="inc_grp")
            xt = ps_xt.tile([P, 2 * EP, P], F32, tag="xt")
            words = inc_raw[j][:, a, :].bitcast(F32)
            for g in range(EP):
                for u in range(2):
                    nc.tensor.transpose(xt[:, 2 * g + u, :], words[:, 256 * g + u : 256 * (g + 1) : 2], ident[:])
            nc.scalar.copy(
                out=inc_grp[j][:, a].bitcast(F32),
                in_=xt[:].rearrange("p (g u) n -> p g n u", u=2),
            )

        def transpose_pair(j):
            for a in range(GT):
                transpose_tile(j, a)

        def quantise_inc(j):
            codes = work.tile([P, GT, EP, P], U32, tag="inc_codes", align_bytes=64)
            scales = work.tile([P, GT, EP, P], U8, tag="inc_scales", align_bytes=64)
            inc_codes[j] = codes
            inc_scales[j] = scales
            nc.vector.quantize_mx(
                out=codes[:].rearrange("p a g n -> p (a g n)").bitcast(FP8X4),
                scales=scales[:].rearrange("p a g n -> p (a g n)"),
                in_=inc_grp[j][:].rearrange("p a g n t -> p (a g n t)"),
            )

        def stage1(j):
            grp = work.tile([P, GT, P, 4], BF16, tag="prop_grp", align_bytes=64)
            prop_grp[j] = grp
            for a in range(GT):
                pt = ps_pt.tile([P, CT, P], F32, tag="pt")
                for t in range(CT):
                    for g in range(EP):
                        nc.tensor.matmul_mx(
                            out=pt[:, t, :],
                            lhsT=he_codes[:, g, P * t : P * (t + 1)].bitcast(FP8X4),
                            lhsT_scale=he_scales[:, g, P * t : P * (t + 1)],
                            rhs=inc_codes[j][:, a, g, :].bitcast(FP8X4),
                            rhs_scale=inc_scales[j][:, a, g, :],
                            start=(g == 0),
                            stop=(g == EP - 1),
                        )
                nc.scalar.copy(out=grp[:, a], in_=pt[:].rearrange("p t n -> p n t"))

        def quantise_prop(j):
            codes = work.tile([P, GT, P], U32, tag="prop_codes", align_bytes=64)
            scales = work.tile([P, GT, P], U8, tag="prop_scales", align_bytes=64)
            prop_codes[j] = codes
            prop_scales[j] = scales
            nc.vector.quantize_mx(
                out=codes[:].rearrange("p a n -> p (a n)").bitcast(FP8X4),
                scales=scales[:].rearrange("p a n -> p (a n)"),
                in_=prop_grp[j][:].rearrange("p a n t -> p (a n t)"),
            )

        def stage2(j):
            out_ps[j] = []
            for a in range(GT):
                po = ps_po.tile([P, C], F32, tag="po")
                nc.tensor.matmul_mx(
                    out=po[:],
                    lhsT=prop_codes[j][:, a, :].bitcast(FP8X4),
                    lhsT_scale=prop_scales[j][:, a, :],
                    rhs=w2_codes[:].bitcast(FP8X4),
                    rhs_scale=w2_scales[:],
                    start=True,
                    stop=True,
                )
                out_ps[j].append(po)

        def pre_add_on_tensor(j, a):
            k, h = divmod(j, 2)
            ps = ps_xt.tile([P, C], F32, tag="xt")
            nc.tensor.matmul(ps[:], lhsT=ident16[:], rhs=nf_raw[k][:, GT * h + a, :], start=True, stop=False)
            nc.tensor.matmul(ps[:], lhsT=ones[:], rhs=b2pad[:], start=False, stop=True)
            nc.scalar.copy(out=nfb[j][:, a, :], in_=ps[:])

        def pre_add(j, a0, a1):
            k, h = divmod(j, 2)
            nc.vector.tensor_tensor(
                out=nfb[j][:, a0:a1, :],
                in0=nf_raw[k][:, GT * h + a0 : GT * h + a1, :],
                in1=b2bc[:].unsqueeze(1).to_broadcast([P, a1 - a0, C]),
                op=ADD,
            )

        res = {}

        def finish_tile(j, a):
            if a == 0:
                res[j] = const.tile([P, GT, C], F32, name="res%d" % j)
            nc.vector.tensor_tensor(out=res[j][:, a, :], in0=out_ps[j][a][:], in1=nfb[j][:, a, :], op=ADD)
            if j >= NG - 2:
                nc.sync.dma_start(out=out_v[:, GT * j + a, :], in_=res[j][:, a, :])
            elif a == GT - 1:
                nc.sync.dma_start(out=out_v[:, GT * j : GT * (j + 1), :], in_=res[j][:])

        warm_up(4)
        transpose_tile(0, 0)
        warm_up(2)
        regroup_he(nc.scalar.copy, 1, 80, P)
        spread_bias()
        transpose_tile(0, 1)
        regroup_he(nc.vector.tensor_copy, 0, 0, P)
        regroup_he(nc.vector.tensor_copy, 1, 0, 80)
        quantise_he(0)
        quantise_he(1)
        quantise_inc(0)
        transpose_pair(1)
        stage1(0)
        regroup_w2()
        quantise_inc(1)
        quantise_w2()
        quantise_prop(0)
        for j in range(NG + 2):
            if 0 < j < NG:
                stage1(j)
            if j + 2 < NG:
                transpose_pair(j + 2)
            if 0 < j <= NG:
                stage2(j - 1)
            if j < NG:
                nfb[j] = const.tile([P, GT, C], F32, name="nfb%d" % j)
                on_vector = GT - ON_TENSOR.get(j, 0)
                for a in range(on_vector, GT):
                    pre_add_on_tensor(j, a)
            if 0 < j and j + 1 < NG:
                quantise_inc(j + 1)
            if j >= 2:
                for a in range(1 if j == NG else 0, GT):
                    finish_tile(j - 2, a)
            if j < NG and on_vector:
                pre_add(j, 0, on_vector)
            if j == NG - 1:
                finish_tile(j - 1, 0)
            if 0 < j < NG:
                quantise_prop(j)
